import numpy as np
import ml_dtypes


def mxq(x, axis, fmt="e4m3"):
    dtype, down = {"e4m3": (ml_dtypes.float8_e4m3fn, 7), "e5m2": (ml_dtypes.float8_e5m2, 14)}[fmt]
    v = np.moveaxis(np.asarray(x, np.float32).astype(ml_dtypes.bfloat16).astype(np.float64), axis, -1)
    blocks = v.reshape(v.shape[:-1] + (-1, 32))
    amax = np.abs(blocks).max(-1, keepdims=True)
    byte = np.maximum(np.where(amax > 0, np.frexp(amax)[1] - 1 + 127, 0) - down, 1)
    scale = np.exp2(byte - 127.0)
    codes = (blocks / scale).astype(np.float32).astype(dtype).astype(np.float64)
    return np.moveaxis((codes * scale).reshape(v.shape), -1, axis)


WIDE = False


def mx_kscale(k):
    if not WIDE:
        return np.ones(k)
    levels = np.array([10, -10, 5, -5, 0])
    a = np.random.permutation(np.resize(levels, k // 512 * 4)).reshape(k // 512, 4)
    idx = np.arange(k)
    return np.exp2(a[idx // 512, idx % 128 // 32])


BF16 = ml_dtypes.bfloat16


def bf(x):
    return np.asarray(x, np.float32).astype(BF16)


def f64(x):
    return np.asarray(x).astype(np.float64)


B, L, F, D, N = 16, 1024, 512, 512, 8192
TOP = 0.8 * np.sqrt(2.0 * np.log(L))


def elu(v):
    return np.where(v > 0.0, v, np.exp(np.minimum(v, 0.0)) - 1.0)


def setup_inputs():
    s = mx_kscale(F)
    return {"x": bf(np.random.standard_normal((B, L, F)) * s),
            "conv_w": bf(np.random.standard_normal((D, F)) / np.sqrt(F) / s),
            "conv_b": bf(np.random.standard_normal(D) * 2.0 - TOP)}


def reference(x, conv_w, conv_b):
    z = (mxq(f64(x), 2, "e4m3") @ mxq(f64(conv_w), 1, "e4m3").T) + f64(conv_b)
    return elu(z).max(axis=1)

@@ -1,0 +1,180 @@
+from contextlib import ExitStack
+
+import concourse.mybir as mybir
+from concourse.masks import make_identity
+
+F32 = mybir.dt.float32
+BF16 = mybir.dt.bfloat16
+U32 = mybir.dt.uint32
+U8 = mybir.dt.uint8
+FP8X4 = mybir.dt.float8_e4m3fn_x4
+ALU = mybir.AluOpType
+
+P = 128
+PACK = 4
+FEATURES = P * PACK
+WORDS = FEATURES // 2
+BATCH = 16
+POSITIONS = 1024
+CHANNELS = 512
+CHANNEL_TILES = CHANNELS // P
+CHUNK = 512
+CHUNK_ROW_TILES = CHUNK // P
+CHUNKS_PER_SEQ = POSITIONS // CHUNK
+N_CHUNKS = BATCH * CHUNKS_PER_SEQ
+PAIR = 2 * P
+
+FLOPS = 2 * BATCH * POSITIONS * FEATURES * CHANNELS
+
+
+def flip_rows(nc, psum_flip, ident, rows, grouped, n_row_tiles):
+    row_words = rows.bitcast(F32)
+    grouped_words = grouped.bitcast(F32)
+    for pair in range(n_row_tiles // 2):
+        flipped = psum_flip.tile([P, 2, PAIR], F32, name="flipped")
+        for s in range(2):
+            for u in range(2):
+                nc.tensor.transpose(
+                    flipped[:, u, s * P : (s + 1) * P],
+                    row_words[:, 2 * pair + s, u * P : (u + 1) * P],
+                    ident,
+                )
+        nc.scalar.copy(
+            out=grouped_words[:, pair * PAIR : (pair + 1) * PAIR, :],
+            in_=flipped[:].rearrange("p u r -> p r u"),
+        )
+
+
+def quantise(nc, grouped, codes, scales):
+    nc.vector.quantize_mx(
+        out=codes.bitcast(FP8X4),
+        scales=scales,
+        in_=grouped.rearrange("p r j -> p (r j)"),
+    )
+
+
+def tile_conceptembedmodel_pa_t_kernel(tc, x, conv_w, conv_b, out):
+    nc = tc.nc
+    x_rows = x.flatten_outer_dims()
+
+    with ExitStack() as ctx:
+        consts = ctx.enter_context(tc.tile_pool(name="consts", bufs=1))
+        x_pool = ctx.enter_context(tc.tile_pool(name="x_pool", bufs=N_CHUNKS))
+        stage = ctx.enter_context(tc.tile_pool(name="stage", bufs=3))
+        psum_flip = ctx.enter_context(tc.psum_pool(name="psum_flip", bufs=4))
+        psum_acc = ctx.enter_context(tc.psum_pool(name="psum_acc", bufs=4))
+        ctx.enter_context(tc.manual_schedule())
+
+        w_rows = consts.tile([P, CHANNEL_TILES, FEATURES], BF16)
+        nc.sync.dma_start(out=w_rows[:], in_=conv_w.rearrange("(t p) f -> p t f", p=P))
+        x_chunks = []
+        for c in range(N_CHUNKS):
+            x_chunk = x_pool.tile([P, CHUNK_ROW_TILES, FEATURES], BF16, name="x_chunk")
+            nc.sync.dma_start(
+                out=x_chunk[:],
+                in_=x_rows[c * CHUNK : (c + 1) * CHUNK, :].rearrange(
+                    "(p j) f -> p j f", j=CHUNK_ROW_TILES
+                ),
+            )
+            x_chunks.append(x_chunk)
+        bias_rows = consts.tile([P, P], BF16)
+        nc.vector.memset(bias_rows[:], 0.0)
+        nc.scalar.dma_start(
+            out=bias_rows[0:CHANNEL_TILES, :], in_=conv_b.rearrange("(t j) -> t j", j=P)
+        )
+
+        ident = consts.tile([P, P], F32)
+        make_identity(nc, ident[:])
+        warm = consts.tile([P, 1], F32)
+        nc.vector.memset(warm[:], 0.0)
+        nc.scalar.activation(out=warm[:], in_=warm[:], func=mybir.ActivationFunctionType.Exp)
+        result = consts.tile([P, P], F32)
+        nc.vector.memset(result[:], 0.0)
+        bias_rows_f32 = consts.tile([P, P], F32)
+        nc.vector.tensor_copy(out=bias_rows_f32[:], in_=bias_rows[:])
+
+        w_grouped = consts.tile([P, CHANNELS, PACK], BF16, align_bytes=64)
+        w_codes = consts.tile([P, CHANNELS], U32, align_bytes=64)
+        w_scales = consts.tile([P, CHANNELS], U8, align_bytes=64)
+        flip_rows(nc, psum_flip, ident[:], w_rows[:], w_grouped[:], CHANNEL_TILES)
+        quantise(nc, w_grouped[:], w_codes[:], w_scales[:])
+
+        grouped_of = {}
+        codes_of = {}
+        scales_of = {}
+        chunk_max = consts.tile([P, N_CHUNKS, CHANNEL_TILES], F32)
+
+        def flip_chunk(c):
+            grouped_of[c] = stage.tile([P, CHUNK, PACK], BF16, align_bytes=64, name="x_grouped")
+            flip_rows(nc, psum_flip, ident[:], x_chunks[c][:], grouped_of[c][:], CHUNK_ROW_TILES)
+
+        def quantise_chunk(c):
+            codes_of[c] = stage.tile([P, CHUNK], U32, align_bytes=64, name="x_codes")
+            scales_of[c] = stage.tile([P, CHUNK], U8, align_bytes=64, name="x_scales")
+            quantise(nc, grouped_of[c][:], codes_of[c][:], scales_of[c][:])
+
+        def multiply_chunk(c):
+            for t in range(CHANNEL_TILES):
+                channels = slice(t * P, (t + 1) * P)
+                acc = psum_acc.tile([P, CHUNK], F32, name="acc")
+                nc.tensor.matmul_mx(
+                    out=acc[:],
+                    lhsT=w_codes[:, channels].bitcast(FP8X4),
+                    lhsT_scale=w_scales[:, channels],
+                    rhs=codes_of[c][:].bitcast(FP8X4),
+                    rhs_scale=scales_of[c][:],
+                    start=True,
+                    stop=True,
+                )
+                nc.vector.tensor_reduce(
+                    out=chunk_max[:, c, t : t + 1],
+                    in_=acc[:],
+                    axis=mybir.AxisListType.X,
+                    op=ALU.max,
+                )
+
+        flip_chunk(0)
+        flip_chunk(1)
+        quantise_chunk(0)
+        bias_flipped = psum_flip.tile([P, 2, PAIR], F32, name="flipped")
+        nc.tensor.transpose(bias_flipped[:, 0, 0:P], bias_rows_f32[:], ident[:])
+        bias_col = consts.tile([P, CHANNEL_TILES], F32)
+        nc.scalar.copy(out=bias_col[:], in_=bias_flipped[:, 0, 0:CHANNEL_TILES])
+        for c in range(N_CHUNKS):
+            if c + 2 < N_CHUNKS:
+                flip_chunk(c + 2)
+            if c + 1 < N_CHUNKS:
+                quantise_chunk(c + 1)
+            multiply_chunk(c)
+
+        halves = chunk_max[:].rearrange("p (b h) t -> p b h t", h=CHUNKS_PER_SEQ)
+        shape = [P, BATCH, CHANNEL_TILES]
+        v = consts.tile(shape, F32)
+        nc.vector.tensor_tensor(out=v[:], in0=halves[:, :, 0, :], in1=halves[:, :, 1, :], op=ALU.max)
+        nc.vector.tensor_tensor(
+            out=v[:], in0=v[:], in1=bias_col[:].unsqueeze(1).to_broadcast(shape), op=ALU.add
+        )
+        negative = consts.tile(shape, F32)
+        nc.vector.tensor_scalar_min(out=negative[:], in0=v[:], scalar1=0.0)
+        nc.scalar.activation(
+            out=negative[:], in_=negative[:], func=mybir.ActivationFunctionType.Exp
+        )
+        positive = consts.tile(shape, F32)
+        nc.vector.tensor_scalar_max(out=positive[:], in0=v[:], scalar1=0.0)
+        nc.vector.scalar_tensor_tensor(
+            out=result[:, 0 : BATCH * CHANNEL_TILES],
+            in0=negative[:].rearrange("p b t -> p (b t)"),
+            scalar=-1.0,
+            in1=positive[:].rearrange("p b t -> p (b t)"),
+            op0=ALU.add,
+            op1=ALU.add,
+        )
+
+        result_flipped = psum_flip.tile([P, 2, PAIR], F32, name="flipped")
+        nc.tensor.transpose(result_flipped[:, 0, 0:P], result[:], ident[:])
+        out_rows = consts.tile([P, P], F32)
+        nc.scalar.copy(out=out_rows[:], in_=result_flipped[:, 0, 0:P])
+        nc.sync.dma_start(
+            out=out.rearrange("b (t j) -> (b t) j", j=P),
+            in_=out_rows[0 : BATCH * CHANNEL_TILES, :],
+        )

@@ -9,20 +9,21 @@ U32 = mybir.dt.uint32
 U8 = mybir.dt.uint8
 FP8X4 = mybir.dt.float8_e4m3fn_x4
 ALU = mybir.AluOpType
+FUNC = mybir.ActivationFunctionType
 
 P = 128
 PACK = 4
 FEATURES = P * PACK
-WORDS = FEATURES // 2
 BATCH = 16
 POSITIONS = 1024
 CHANNELS = 512
 CHANNEL_TILES = CHANNELS // P
 CHUNK = 512
 CHUNK_ROW_TILES = CHUNK // P
-CHUNKS_PER_SEQ = POSITIONS // CHUNK
-N_CHUNKS = BATCH * CHUNKS_PER_SEQ
+N_CHUNKS = BATCH * POSITIONS // CHUNK
 PAIR = 2 * P
+N_PAIRED = 1
+N_PLAIN = CHANNEL_TILES - N_PAIRED
 
 FLOPS = 2 * BATCH * POSITIONS * FEATURES * CHANNELS
 
@@ -60,9 +61,12 @@ def tile_conceptembedmodel_pa_t_kernel(tc, x, conv_w, conv_b, out):
     with ExitStack() as ctx:
         consts = ctx.enter_context(tc.tile_pool(name="consts", bufs=1))
         x_pool = ctx.enter_context(tc.tile_pool(name="x_pool", bufs=N_CHUNKS))
-        stage = ctx.enter_context(tc.tile_pool(name="stage", bufs=3))
-        psum_flip = ctx.enter_context(tc.psum_pool(name="psum_flip", bufs=4))
-        psum_acc = ctx.enter_context(tc.psum_pool(name="psum_acc", bufs=4))
+        stage = ctx.enter_context(tc.tile_pool(name="stage", bufs=4))
+        pair_in = ctx.enter_context(tc.tile_pool(name="pair_in", bufs=2))
+        pair_out = ctx.enter_context(tc.tile_pool(name="pair_out", bufs=1))
+        psum_flip = ctx.enter_context(tc.psum_pool(name="psum_flip", bufs=3))
+        psum_acc = ctx.enter_context(tc.psum_pool(name="psum_acc", bufs=3))
+        psum_pair = ctx.enter_context(tc.psum_pool(name="psum_pair", bufs=2))
         ctx.enter_context(tc.manual_schedule())
 
         w_rows = consts.tile([P, CHANNEL_TILES, FEATURES], BF16)
@@ -87,7 +91,7 @@ def tile_conceptembedmodel_pa_t_kernel(tc, x, conv_w, conv_b, out):
         make_identity(nc, ident[:])
         warm = consts.tile([P, 1], F32)
         nc.vector.memset(warm[:], 0.0)
-        nc.scalar.activation(out=warm[:], in_=warm[:], func=mybir.ActivationFunctionType.Exp)
+        nc.scalar.activation(out=warm[:], in_=warm[:], func=FUNC.Exp)
         result = consts.tile([P, P], F32)
         nc.vector.memset(result[:], 0.0)
         bias_rows_f32 = consts.tile([P, P], F32)
@@ -98,11 +102,22 @@ def tile_conceptembedmodel_pa_t_kernel(tc, x, conv_w, conv_b, out):
         w_scales = consts.tile([P, CHANNELS], U8, align_bytes=64)
         flip_rows(nc, psum_flip, ident[:], w_rows[:], w_grouped[:], CHANNEL_TILES)
         quantise(nc, w_grouped[:], w_codes[:], w_scales[:])
+        neg_grouped = consts.tile([P, N_PAIRED * P, PACK], BF16, align_bytes=64)
+        neg_codes = consts.tile([P, N_PAIRED * P], U32, align_bytes=64)
+        neg_scales = consts.tile([P, N_PAIRED * P], U8, align_bytes=64)
+        nc.vector.tensor_scalar_mul(
+            out=neg_grouped[:], in0=w_grouped[:, N_PLAIN * P :, :], scalar1=-1.0
+        )
+        quantise(nc, neg_grouped[:], neg_codes[:], neg_scales[:])
 
         grouped_of = {}
         codes_of = {}
         scales_of = {}
-        chunk_max = consts.tile([P, N_CHUNKS, CHANNEL_TILES], F32)
+        excess_of = {}
+        second_of = {}
+        larger_of = {}
+        plain_max = consts.tile([P, N_CHUNKS, N_PLAIN], F32)
+        seq_max = consts.tile([P, BATCH, CHANNEL_TILES], F32)
 
         def flip_chunk(c):
             grouped_of[c] = stage.tile([P, CHUNK, PACK], BF16, align_bytes=64, name="x_grouped")
@@ -113,52 +128,94 @@ def tile_conceptembedmodel_pa_t_kernel(tc, x, conv_w, conv_b, out):
             scales_of[c] = stage.tile([P, CHUNK], U8, align_bytes=64, name="x_scales")
             quantise(nc, grouped_of[c][:], codes_of[c][:], scales_of[c][:])
 
-        def multiply_chunk(c):
-            for t in range(CHANNEL_TILES):
+        def mx_pass(acc, weight_codes, weight_scales, c, start, stop):
+            nc.tensor.matmul_mx(
+                out=acc,
+                lhsT=weight_codes.bitcast(FP8X4),
+                lhsT_scale=weight_scales,
+                rhs=codes_of[c][:].bitcast(FP8X4),
+                rhs_scale=scales_of[c][:],
+                start=start,
+                stop=stop,
+            )
+
+        def multiply_plain(c):
+            for t in range(N_PLAIN):
                 channels = slice(t * P, (t + 1) * P)
                 acc = psum_acc.tile([P, CHUNK], F32, name="acc")
-                nc.tensor.matmul_mx(
-                    out=acc[:],
-                    lhsT=w_codes[:, channels].bitcast(FP8X4),
-                    lhsT_scale=w_scales[:, channels],
-                    rhs=codes_of[c][:].bitcast(FP8X4),
-                    rhs_scale=scales_of[c][:],
-                    start=True,
-                    stop=True,
-                )
+                mx_pass(acc[:], w_codes[:, channels], w_scales[:, channels], c, True, True)
                 nc.vector.tensor_reduce(
-                    out=chunk_max[:, c, t : t + 1],
+                    out=plain_max[:, c, t : t + 1],
                     in_=acc[:],
                     axis=mybir.AxisListType.X,
                     op=ALU.max,
                 )
 
-        flip_chunk(0)
-        flip_chunk(1)
+        def multiply_paired(b):
+            first, second = 2 * b, 2 * b + 1
+            excess_of[b] = pair_in.tile([P, N_PAIRED, CHUNK], F32, name="excess")
+            second_of[b] = pair_in.tile([P, N_PAIRED, CHUNK], F32, name="second_products")
+            for i in range(N_PAIRED):
+                channels = slice((N_PLAIN + i) * P, (N_PLAIN + i + 1) * P)
+                negated = slice(i * P, (i + 1) * P)
+                difference = psum_pair.tile([P, CHUNK], F32, name="pair_bank")
+                mx_pass(difference[:], w_codes[:, channels], w_scales[:, channels], first, True, False)
+                mx_pass(difference[:], neg_codes[:, negated], neg_scales[:, negated], second, False, True)
+                products = psum_pair.tile([P, CHUNK], F32, name="pair_bank")
+                mx_pass(products[:], w_codes[:, channels], w_scales[:, channels], second, True, True)
+                nc.scalar.activation(out=excess_of[b][:, i, :], in_=difference[:], func=FUNC.Relu)
+                nc.scalar.copy(out=second_of[b][:, i, :], in_=products[:])
+
+        def add_paired(b):
+            larger_of[b] = pair_out.tile([P, N_PAIRED, CHUNK], F32, name="larger")
+            nc.gpsimd.tensor_tensor(
+                out=larger_of[b][:], in0=second_of[b][:], in1=excess_of[b][:], op=ALU.add
+            )
+
+        def reduce_paired(b):
+            nc.vector.tensor_reduce(
+                out=seq_max[:, b, N_PLAIN:],
+                in_=larger_of[b][:],
+                axis=mybir.AxisListType.X,
+                op=ALU.max,
+            )
+
+        for c in range(4):
+            flip_chunk(c)
         quantise_chunk(0)
+        quantise_chunk(1)
         bias_flipped = psum_flip.tile([P, 2, PAIR], F32, name="flipped")
         nc.tensor.transpose(bias_flipped[:, 0, 0:P], bias_rows_f32[:], ident[:])
         bias_col = consts.tile([P, CHANNEL_TILES], F32)
         nc.scalar.copy(out=bias_col[:], in_=bias_flipped[:, 0, 0:CHANNEL_TILES])
-        for c in range(N_CHUNKS):
-            if c + 2 < N_CHUNKS:
-                flip_chunk(c + 2)
-            if c + 1 < N_CHUNKS:
-                quantise_chunk(c + 1)
-            multiply_chunk(c)
+        for b in range(BATCH):
+            multiply_plain(2 * b)
+            multiply_paired(b)
+            if b + 2 < BATCH:
+                flip_chunk(2 * b + 4)
+            if b + 1 < BATCH:
+                quantise_chunk(2 * b + 2)
+                quantise_chunk(2 * b + 3)
+            if b >= 1:
+                reduce_paired(b - 1)
+            add_paired(b)
+            multiply_plain(2 * b + 1)
+            if b + 2 < BATCH:
+                flip_chunk(2 * b + 5)
+        reduce_paired(BATCH - 1)
 
-        halves = chunk_max[:].rearrange("p (b h) t -> p b h t", h=CHUNKS_PER_SEQ)
+        halves = plain_max[:].rearrange("p (b h) t -> p b h t", h=2)
+        nc.vector.tensor_tensor(
+            out=seq_max[:, :, 0:N_PLAIN], in0=halves[:, :, 0, :], in1=halves[:, :, 1, :], op=ALU.max
+        )
         shape = [P, BATCH, CHANNEL_TILES]
         v = consts.tile(shape, F32)
-        nc.vector.tensor_tensor(out=v[:], in0=halves[:, :, 0, :], in1=halves[:, :, 1, :], op=ALU.max)
         nc.vector.tensor_tensor(
-            out=v[:], in0=v[:], in1=bias_col[:].unsqueeze(1).to_broadcast(shape), op=ALU.add
+            out=v[:], in0=seq_max[:], in1=bias_col[:].unsqueeze(1).to_broadcast(shape), op=ALU.add
         )
         negative = consts.tile(shape, F32)
         nc.vector.tensor_scalar_min(out=negative[:], in0=v[:], scalar1=0.0)
-        nc.scalar.activation(
-            out=negative[:], in_=negative[:], func=mybir.ActivationFunctionType.Exp
-        )
+        nc.scalar.activation(out=negative[:], in_=negative[:], func=FUNC.Exp)
         positive = consts.tile(shape, F32)
         nc.vector.tensor_scalar_max(out=positive[:], in0=v[:], scalar1=0.0)
         nc.vector.scalar_tensor_tensor(

@@ -22,7 +22,7 @@ CHUNK = 512
 CHUNK_ROW_TILES = CHUNK // P
 N_CHUNKS = BATCH * POSITIONS // CHUNK
 PAIR = 2 * P
-N_PAIRED = 1
+N_PAIRED = 2
 N_PLAIN = CHANNEL_TILES - N_PAIRED
 
 FLOPS = 2 * BATCH * POSITIONS * FEATURES * CHANNELS
@@ -62,7 +62,7 @@ def tile_conceptembedmodel_pa_t_kernel(tc, x, conv_w, conv_b, out):
         consts = ctx.enter_context(tc.tile_pool(name="consts", bufs=1))
         x_pool = ctx.enter_context(tc.tile_pool(name="x_pool", bufs=N_CHUNKS))
         stage = ctx.enter_context(tc.tile_pool(name="stage", bufs=4))
-        pair_in = ctx.enter_context(tc.tile_pool(name="pair_in", bufs=2))
+        pair_in = ctx.enter_context(tc.tile_pool(name="pair_in", bufs=4))
         pair_out = ctx.enter_context(tc.tile_pool(name="pair_out", bufs=1))
         psum_flip = ctx.enter_context(tc.psum_pool(name="psum_flip", bufs=3))
         psum_acc = ctx.enter_context(tc.psum_pool(name="psum_acc", bufs=3))
@@ -105,10 +105,6 @@ def tile_conceptembedmodel_pa_t_kernel(tc, x, conv_w, conv_b, out):
         neg_grouped = consts.tile([P, N_PAIRED * P, PACK], BF16, align_bytes=64)
         neg_codes = consts.tile([P, N_PAIRED * P], U32, align_bytes=64)
         neg_scales = consts.tile([P, N_PAIRED * P], U8, align_bytes=64)
-        nc.vector.tensor_scalar_mul(
-            out=neg_grouped[:], in0=w_grouped[:, N_PLAIN * P :, :], scalar1=-1.0
-        )
-        quantise(nc, neg_grouped[:], neg_codes[:], neg_scales[:])
 
         grouped_of = {}
         codes_of = {}
@@ -151,58 +147,68 @@ def tile_conceptembedmodel_pa_t_kernel(tc, x, conv_w, conv_b, out):
                     op=ALU.max,
                 )
 
-        def multiply_paired(b):
+        def multiply_paired(b, i):
             first, second = 2 * b, 2 * b + 1
-            excess_of[b] = pair_in.tile([P, N_PAIRED, CHUNK], F32, name="excess")
-            second_of[b] = pair_in.tile([P, N_PAIRED, CHUNK], F32, name="second_products")
-            for i in range(N_PAIRED):
-                channels = slice((N_PLAIN + i) * P, (N_PLAIN + i + 1) * P)
-                negated = slice(i * P, (i + 1) * P)
-                difference = psum_pair.tile([P, CHUNK], F32, name="pair_bank")
-                mx_pass(difference[:], w_codes[:, channels], w_scales[:, channels], first, True, False)
-                mx_pass(difference[:], neg_codes[:, negated], neg_scales[:, negated], second, False, True)
-                products = psum_pair.tile([P, CHUNK], F32, name="pair_bank")
-                mx_pass(products[:], w_codes[:, channels], w_scales[:, channels], second, True, True)
-                nc.scalar.activation(out=excess_of[b][:, i, :], in_=difference[:], func=FUNC.Relu)
-                nc.scalar.copy(out=second_of[b][:, i, :], in_=products[:])
+            channels = slice((N_PLAIN + i) * P, (N_PLAIN + i + 1) * P)
+            negated = slice(i * P, (i + 1) * P)
+            difference = psum_pair.tile([P, CHUNK], F32, name="pair_bank")
+            mx_pass(difference[:], w_codes[:, channels], w_scales[:, channels], first, True, False)
+            mx_pass(difference[:], neg_codes[:, negated], neg_scales[:, negated], second, False, True)
+            products = psum_pair.tile([P, CHUNK], F32, name="pair_bank")
+            mx_pass(products[:], w_codes[:, channels], w_scales[:, channels], second, True, True)
+            excess_of[b, i] = pair_in.tile([P, CHUNK], F32, name="excess")
+            second_of[b, i] = pair_in.tile([P, CHUNK], F32, name="second_products")
+            nc.scalar.activation(out=excess_of[b, i][:], in_=difference[:], func=FUNC.Relu)
+            nc.scalar.copy(out=second_of[b, i][:], in_=products[:])
 
-        def add_paired(b):
-            larger_of[b] = pair_out.tile([P, N_PAIRED, CHUNK], F32, name="larger")
+        def add_paired(b, i):
+            larger_of[b, i] = pair_out.tile([P, CHUNK], F32, name="larger_%d" % i)
             nc.gpsimd.tensor_tensor(
-                out=larger_of[b][:], in0=second_of[b][:], in1=excess_of[b][:], op=ALU.add
+                out=larger_of[b, i][:], in0=second_of[b, i][:], in1=excess_of[b, i][:], op=ALU.add
             )
 
-        def reduce_paired(b):
+        def reduce_paired(b, i):
             nc.vector.tensor_reduce(
-                out=seq_max[:, b, N_PLAIN:],
-                in_=larger_of[b][:],
+                out=seq_max[:, b, N_PLAIN + i : N_PLAIN + i + 1],
+                in_=larger_of[b, i][:],
                 axis=mybir.AxisListType.X,
                 op=ALU.max,
             )
 
-        for c in range(4):
-            flip_chunk(c)
+        flip_chunk(0)
+        flip_chunk(1)
         quantise_chunk(0)
         quantise_chunk(1)
+        multiply_plain(0)
+        nc.vector.tensor_scalar_mul(
+            out=neg_grouped[:], in0=w_grouped[:, N_PLAIN * P :, :], scalar1=-1.0
+        )
+        quantise(nc, neg_grouped[:], neg_codes[:], neg_scales[:])
+        flip_chunk(2)
+        flip_chunk(3)
         bias_flipped = psum_flip.tile([P, 2, PAIR], F32, name="flipped")
         nc.tensor.transpose(bias_flipped[:, 0, 0:P], bias_rows_f32[:], ident[:])
         bias_col = consts.tile([P, CHANNEL_TILES], F32)
         nc.scalar.copy(out=bias_col[:], in_=bias_flipped[:, 0, 0:CHANNEL_TILES])
         for b in range(BATCH):
-            multiply_plain(2 * b)
-            multiply_paired(b)
+            multiply_paired(b, 0)
             if b + 2 < BATCH:
                 flip_chunk(2 * b + 4)
+            multiply_paired(b, 1)
             if b + 1 < BATCH:
                 quantise_chunk(2 * b + 2)
                 quantise_chunk(2 * b + 3)
-            if b >= 1:
-                reduce_paired(b - 1)
-            add_paired(b)
+            for i in range(N_PAIRED):
+                if b >= 1:
+                    reduce_paired(b - 1, i)
+                add_paired(b, i)
             multiply_plain(2 * b + 1)
             if b + 2 < BATCH:
                 flip_chunk(2 * b + 5)
-        reduce_paired(BATCH - 1)
+            if b + 1 < BATCH:
+                multiply_plain(2 * b + 2)
+        for i in range(N_PAIRED):
+            reduce_paired(BATCH - 1, i)
 
         halves = plain_max[:].rearrange("p (b h) t -> p b h t", h=2)
         nc.vector.tensor_tensor(

@@ -22,17 +22,18 @@ CHUNK = 512
 CHUNK_ROW_TILES = CHUNK // P
 N_CHUNKS = BATCH * POSITIONS // CHUNK
 PAIR = 2 * P
+PSUM_BANKS = 8
 N_PAIRED = 2
 N_PLAIN = CHANNEL_TILES - N_PAIRED
 
 FLOPS = 2 * BATCH * POSITIONS * FEATURES * CHANNELS
 
 
-def flip_rows(nc, psum_flip, ident, rows, grouped, n_row_tiles):
+def flip_rows(nc, psum, ident, rows, grouped, n_row_tiles):
     row_words = rows.bitcast(F32)
     grouped_words = grouped.bitcast(F32)
     for pair in range(n_row_tiles // 2):
-        flipped = psum_flip.tile([P, 2, PAIR], F32, name="flipped")
+        flipped = psum.tile([P, 2, PAIR], F32, name="bank")
         for s in range(2):
             for u in range(2):
                 nc.tensor.transpose(
@@ -64,9 +65,7 @@ def tile_conceptembedmodel_pa_t_kernel(tc, x, conv_w, conv_b, out):
         stage = ctx.enter_context(tc.tile_pool(name="stage", bufs=4))
         pair_in = ctx.enter_context(tc.tile_pool(name="pair_in", bufs=4))
         pair_out = ctx.enter_context(tc.tile_pool(name="pair_out", bufs=1))
-        psum_flip = ctx.enter_context(tc.psum_pool(name="psum_flip", bufs=3))
-        psum_acc = ctx.enter_context(tc.psum_pool(name="psum_acc", bufs=3))
-        psum_pair = ctx.enter_context(tc.psum_pool(name="psum_pair", bufs=2))
+        psum = ctx.enter_context(tc.psum_pool(name="psum", bufs=PSUM_BANKS))
         ctx.enter_context(tc.manual_schedule())
 
         w_rows = consts.tile([P, CHANNEL_TILES, FEATURES], BF16)
@@ -100,7 +99,7 @@ def tile_conceptembedmodel_pa_t_kernel(tc, x, conv_w, conv_b, out):
         w_grouped = consts.tile([P, CHANNELS, PACK], BF16, align_bytes=64)
         w_codes = consts.tile([P, CHANNELS], U32, align_bytes=64)
         w_scales = consts.tile([P, CHANNELS], U8, align_bytes=64)
-        flip_rows(nc, psum_flip, ident[:], w_rows[:], w_grouped[:], CHANNEL_TILES)
+        flip_rows(nc, psum, ident[:], w_rows[:], w_grouped[:], CHANNEL_TILES)
         quantise(nc, w_grouped[:], w_codes[:], w_scales[:])
         neg_grouped = consts.tile([P, N_PAIRED * P, PACK], BF16, align_bytes=64)
         neg_codes = consts.tile([P, N_PAIRED * P], U32, align_bytes=64)
@@ -117,7 +116,7 @@ def tile_conceptembedmodel_pa_t_kernel(tc, x, conv_w, conv_b, out):
 
         def flip_chunk(c):
             grouped_of[c] = stage.tile([P, CHUNK, PACK], BF16, align_bytes=64, name="x_grouped")
-            flip_rows(nc, psum_flip, ident[:], x_chunks[c][:], grouped_of[c][:], CHUNK_ROW_TILES)
+            flip_rows(nc, psum, ident[:], x_chunks[c][:], grouped_of[c][:], CHUNK_ROW_TILES)
 
         def quantise_chunk(c):
             codes_of[c] = stage.tile([P, CHUNK], U32, align_bytes=64, name="x_codes")
@@ -138,7 +137,7 @@ def tile_conceptembedmodel_pa_t_kernel(tc, x, conv_w, conv_b, out):
         def multiply_plain(c):
             for t in range(N_PLAIN):
                 channels = slice(t * P, (t + 1) * P)
-                acc = psum_acc.tile([P, CHUNK], F32, name="acc")
+                acc = psum.tile([P, CHUNK], F32, name="bank")
                 mx_pass(acc[:], w_codes[:, channels], w_scales[:, channels], c, True, True)
                 nc.vector.tensor_reduce(
                     out=plain_max[:, c, t : t + 1],
@@ -151,10 +150,10 @@ def tile_conceptembedmodel_pa_t_kernel(tc, x, conv_w, conv_b, out):
             first, second = 2 * b, 2 * b + 1
             channels = slice((N_PLAIN + i) * P, (N_PLAIN + i + 1) * P)
             negated = slice(i * P, (i + 1) * P)
-            difference = psum_pair.tile([P, CHUNK], F32, name="pair_bank")
+            difference = psum.tile([P, CHUNK], F32, name="bank")
             mx_pass(difference[:], w_codes[:, channels], w_scales[:, channels], first, True, False)
             mx_pass(difference[:], neg_codes[:, negated], neg_scales[:, negated], second, False, True)
-            products = psum_pair.tile([P, CHUNK], F32, name="pair_bank")
+            products = psum.tile([P, CHUNK], F32, name="bank")
             mx_pass(products[:], w_codes[:, channels], w_scales[:, channels], second, True, True)
             excess_of[b, i] = pair_in.tile([P, CHUNK], F32, name="excess")
             second_of[b, i] = pair_in.tile([P, CHUNK], F32, name="second_products")
@@ -186,15 +185,13 @@ def tile_conceptembedmodel_pa_t_kernel(tc, x, conv_w, conv_b, out):
         quantise(nc, neg_grouped[:], neg_codes[:], neg_scales[:])
         flip_chunk(2)
         flip_chunk(3)
-        bias_flipped = psum_flip.tile([P, 2, PAIR], F32, name="flipped")
+        bias_flipped = psum.tile([P, 2, PAIR], F32, name="bank")
         nc.tensor.transpose(bias_flipped[:, 0, 0:P], bias_rows_f32[:], ident[:])
         bias_col = consts.tile([P, CHANNEL_TILES], F32)
         nc.scalar.copy(out=bias_col[:], in_=bias_flipped[:, 0, 0:CHANNEL_TILES])
         for b in range(BATCH):
-            multiply_paired(b, 0)
-            if b + 2 < BATCH:
-                flip_chunk(2 * b + 4)
-            multiply_paired(b, 1)
+            for i in range(N_PAIRED):
+                multiply_paired(b, i)
             if b + 1 < BATCH:
                 quantise_chunk(2 * b + 2)
                 quantise_chunk(2 * b + 3)
@@ -203,10 +200,11 @@ def tile_conceptembedmodel_pa_t_kernel(tc, x, conv_w, conv_b, out):
                     reduce_paired(b - 1, i)
                 add_paired(b, i)
             multiply_plain(2 * b + 1)
-            if b + 2 < BATCH:
-                flip_chunk(2 * b + 5)
             if b + 1 < BATCH:
                 multiply_plain(2 * b + 2)
+            if b + 2 < BATCH:
+                flip_chunk(2 * b + 4)
+                flip_chunk(2 * b + 5)
         for i in range(N_PAIRED):
             reduce_paired(BATCH - 1, i)
 
@@ -233,7 +231,7 @@ def tile_conceptembedmodel_pa_t_kernel(tc, x, conv_w, conv_b, out):
             op1=ALU.add,
         )
 
-        result_flipped = psum_flip.tile([P, 2, PAIR], F32, name="flipped")
+        result_flipped = psum.tile([P, 2, PAIR], F32, name="bank")
         nc.tensor.transpose(result_flipped[:, 0, 0:P], result[:], ident[:])
         out_rows = consts.tile([P, P], F32)
         nc.scalar.copy(out=out_rows[:], in_=result_flipped[:, 0, 0:P])

@@ -64,7 +64,7 @@ def tile_conceptembedmodel_pa_t_kernel(tc, x, conv_w, conv_b, out):
         x_pool = ctx.enter_context(tc.tile_pool(name="x_pool", bufs=N_CHUNKS))
         stage = ctx.enter_context(tc.tile_pool(name="stage", bufs=4))
         pair_in = ctx.enter_context(tc.tile_pool(name="pair_in", bufs=4))
-        pair_out = ctx.enter_context(tc.tile_pool(name="pair_out", bufs=1))
+        pair_out = ctx.enter_context(tc.tile_pool(name="pair_out", bufs=2))
         psum = ctx.enter_context(tc.psum_pool(name="psum", bufs=PSUM_BANKS))
         ctx.enter_context(tc.manual_schedule())
 

from contextlib import ExitStack

import concourse.mybir as mybir
from concourse.masks import make_identity

F32 = mybir.dt.float32
BF16 = mybir.dt.bfloat16
U32 = mybir.dt.uint32
U8 = mybir.dt.uint8
FP8X4 = mybir.dt.float8_e4m3fn_x4
ALU = mybir.AluOpType
FUNC = mybir.ActivationFunctionType

P = 128
PACK = 4
FEATURES = P * PACK
BATCH = 16
POSITIONS = 1024
CHANNELS = 512
CHANNEL_TILES = CHANNELS // P
CHUNK = 512
CHUNK_ROW_TILES = CHUNK // P
N_CHUNKS = BATCH * POSITIONS // CHUNK
PAIR = 2 * P
PSUM_BANKS = 8
N_PAIRED = 2
N_PLAIN = CHANNEL_TILES - N_PAIRED

FLOPS = 2 * BATCH * POSITIONS * FEATURES * CHANNELS


def flip_rows(nc, psum, ident, rows, grouped, n_row_tiles):
    row_words = rows.bitcast(F32)
    grouped_words = grouped.bitcast(F32)
    for pair in range(n_row_tiles // 2):
        flipped = psum.tile([P, 2, PAIR], F32, name="bank")
        for s in range(2):
            for u in range(2):
                nc.tensor.transpose(
                    flipped[:, u, s * P : (s + 1) * P],
                    row_words[:, 2 * pair + s, u * P : (u + 1) * P],
                    ident,
                )
        nc.scalar.copy(
            out=grouped_words[:, pair * PAIR : (pair + 1) * PAIR, :],
            in_=flipped[:].rearrange("p u r -> p r u"),
        )


def quantise(nc, grouped, codes, scales):
    nc.vector.quantize_mx(
        out=codes.bitcast(FP8X4),
        scales=scales,
        in_=grouped.rearrange("p r j -> p (r j)"),
    )


def tile_conceptembedmodel_pa_t_kernel(tc, x, conv_w, conv_b, out):
    nc = tc.nc
    x_rows = x.flatten_outer_dims()

    with ExitStack() as ctx:
        consts = ctx.enter_context(tc.tile_pool(name="consts", bufs=1))
        x_pool = ctx.enter_context(tc.tile_pool(name="x_pool", bufs=N_CHUNKS))
        stage = ctx.enter_context(tc.tile_pool(name="stage", bufs=4))
        pair_in = ctx.enter_context(tc.tile_pool(name="pair_in", bufs=4))
        pair_out = ctx.enter_context(tc.tile_pool(name="pair_out", bufs=2))
        psum = ctx.enter_context(tc.psum_pool(name="psum", bufs=PSUM_BANKS))
        ctx.enter_context(tc.manual_schedule())

        w_rows = consts.tile([P, CHANNEL_TILES, FEATURES], BF16)
        nc.sync.dma_start(out=w_rows[:], in_=conv_w.rearrange("(t p) f -> p t f", p=P))
        x_chunks = []
        for c in range(N_CHUNKS):
            x_chunk = x_pool.tile([P, CHUNK_ROW_TILES, FEATURES], BF16, name="x_chunk")
            nc.sync.dma_start(
                out=x_chunk[:],
                in_=x_rows[c * CHUNK : (c + 1) * CHUNK, :].rearrange(
                    "(p j) f -> p j f", j=CHUNK_ROW_TILES
                ),
            )
            x_chunks.append(x_chunk)
        bias_rows = consts.tile([P, P], BF16)
        nc.vector.memset(bias_rows[:], 0.0)
        nc.scalar.dma_start(
            out=bias_rows[0:CHANNEL_TILES, :], in_=conv_b.rearrange("(t j) -> t j", j=P)
        )

        ident = consts.tile([P, P], F32)
        make_identity(nc, ident[:])
        warm = consts.tile([P, 1], F32)
        nc.vector.memset(warm[:], 0.0)
        nc.scalar.activation(out=warm[:], in_=warm[:], func=FUNC.Exp)
        result = consts.tile([P, P], F32)
        nc.vector.memset(result[:], 0.0)
        bias_rows_f32 = consts.tile([P, P], F32)
        nc.vector.tensor_copy(out=bias_rows_f32[:], in_=bias_rows[:])

        w_grouped = consts.tile([P, CHANNELS, PACK], BF16, align_bytes=64)
        w_codes = consts.tile([P, CHANNELS], U32, align_bytes=64)
        w_scales = consts.tile([P, CHANNELS], U8, align_bytes=64)
        flip_rows(nc, psum, ident[:], w_rows[:], w_grouped[:], CHANNEL_TILES)
        quantise(nc, w_grouped[:], w_codes[:], w_scales[:])
        neg_grouped = consts.tile([P, N_PAIRED * P, PACK], BF16, align_bytes=64)
        neg_codes = consts.tile([P, N_PAIRED * P], U32, align_bytes=64)
        neg_scales = consts.tile([P, N_PAIRED * P], U8, align_bytes=64)

        grouped_of = {}
        codes_of = {}
        scales_of = {}
        excess_of = {}
        second_of = {}
        larger_of = {}
        plain_max = consts.tile([P, N_CHUNKS, N_PLAIN], F32)
        seq_max = consts.tile([P, BATCH, CHANNEL_TILES], F32)

        def flip_chunk(c):
            grouped_of[c] = stage.tile([P, CHUNK, PACK], BF16, align_bytes=64, name="x_grouped")
            flip_rows(nc, psum, ident[:], x_chunks[c][:], grouped_of[c][:], CHUNK_ROW_TILES)

        def quantise_chunk(c):
            codes_of[c] = stage.tile([P, CHUNK], U32, align_bytes=64, name="x_codes")
            scales_of[c] = stage.tile([P, CHUNK], U8, align_bytes=64, name="x_scales")
            quantise(nc, grouped_of[c][:], codes_of[c][:], scales_of[c][:])

        def mx_pass(acc, weight_codes, weight_scales, c, start, stop):
            nc.tensor.matmul_mx(
                out=acc,
                lhsT=weight_codes.bitcast(FP8X4),
                lhsT_scale=weight_scales,
                rhs=codes_of[c][:].bitcast(FP8X4),
                rhs_scale=scales_of[c][:],
                start=start,
                stop=stop,
            )

        def multiply_plain(c):
            for t in range(N_PLAIN):
                channels = slice(t * P, (t + 1) * P)
                acc = psum.tile([P, CHUNK], F32, name="bank")
                mx_pass(acc[:], w_codes[:, channels], w_scales[:, channels], c, True, True)
                nc.vector.tensor_reduce(
                    out=plain_max[:, c, t : t + 1],
                    in_=acc[:],
                    axis=mybir.AxisListType.X,
                    op=ALU.max,
                )

        def multiply_paired(b, i):
            first, second = 2 * b, 2 * b + 1
            channels = slice((N_PLAIN + i) * P, (N_PLAIN + i + 1) * P)
            negated = slice(i * P, (i + 1) * P)
            difference = psum.tile([P, CHUNK], F32, name="bank")
            mx_pass(difference[:], w_codes[:, channels], w_scales[:, channels], first, True, False)
            mx_pass(difference[:], neg_codes[:, negated], neg_scales[:, negated], second, False, True)
            products = psum.tile([P, CHUNK], F32, name="bank")
            mx_pass(products[:], w_codes[:, channels], w_scales[:, channels], second, True, True)
            excess_of[b, i] = pair_in.tile([P, CHUNK], F32, name="excess")
            second_of[b, i] = pair_in.tile([P, CHUNK], F32, name="second_products")
            nc.scalar.activation(out=excess_of[b, i][:], in_=difference[:], func=FUNC.Relu)
            nc.scalar.copy(out=second_of[b, i][:], in_=products[:])

        def add_paired(b, i):
            larger_of[b, i] = pair_out.tile([P, CHUNK], F32, name="larger_%d" % i)
            nc.gpsimd.tensor_tensor(
                out=larger_of[b, i][:], in0=second_of[b, i][:], in1=excess_of[b, i][:], op=ALU.add
            )

        def reduce_paired(b, i):
            nc.vector.tensor_reduce(
                out=seq_max[:, b, N_PLAIN + i : N_PLAIN + i + 1],
                in_=larger_of[b, i][:],
                axis=mybir.AxisListType.X,
                op=ALU.max,
            )

        flip_chunk(0)
        flip_chunk(1)
        quantise_chunk(0)
        quantise_chunk(1)
        multiply_plain(0)
        nc.vector.tensor_scalar_mul(
            out=neg_grouped[:], in0=w_grouped[:, N_PLAIN * P :, :], scalar1=-1.0
        )
        quantise(nc, neg_grouped[:], neg_codes[:], neg_scales[:])
        flip_chunk(2)
        flip_chunk(3)
        bias_flipped = psum.tile([P, 2, PAIR], F32, name="bank")
        nc.tensor.transpose(bias_flipped[:, 0, 0:P], bias_rows_f32[:], ident[:])
        bias_col = consts.tile([P, CHANNEL_TILES], F32)
        nc.scalar.copy(out=bias_col[:], in_=bias_flipped[:, 0, 0:CHANNEL_TILES])
        for b in range(BATCH):
            for i in range(N_PAIRED):
                multiply_paired(b, i)
            if b + 1 < BATCH:
                quantise_chunk(2 * b + 2)
                quantise_chunk(2 * b + 3)
            for i in range(N_PAIRED):
                if b >= 1:
                    reduce_paired(b - 1, i)
                add_paired(b, i)
            multiply_plain(2 * b + 1)
            if b + 1 < BATCH:
                multiply_plain(2 * b + 2)
            if b + 2 < BATCH:
                flip_chunk(2 * b + 4)
                flip_chunk(2 * b + 5)
        for i in range(N_PAIRED):
            reduce_paired(BATCH - 1, i)

        halves = plain_max[:].rearrange("p (b h) t -> p b h t", h=2)
        nc.vector.tensor_tensor(
            out=seq_max[:, :, 0:N_PLAIN], in0=halves[:, :, 0, :], in1=halves[:, :, 1, :], op=ALU.max
        )
        shape = [P, BATCH, CHANNEL_TILES]
        v = consts.tile(shape, F32)
        nc.vector.tensor_tensor(
            out=v[:], in0=seq_max[:], in1=bias_col[:].unsqueeze(1).to_broadcast(shape), op=ALU.add
        )
        negative = consts.tile(shape, F32)
        nc.vector.tensor_scalar_min(out=negative[:], in0=v[:], scalar1=0.0)
        nc.scalar.activation(out=negative[:], in_=negative[:], func=FUNC.Exp)
        positive = consts.tile(shape, F32)
        nc.vector.tensor_scalar_max(out=positive[:], in0=v[:], scalar1=0.0)
        nc.vector.scalar_tensor_tensor(
            out=result[:, 0 : BATCH * CHANNEL_TILES],
            in0=negative[:].rearrange("p b t -> p (b t)"),
            scalar=-1.0,
            in1=positive[:].rearrange("p b t -> p (b t)"),
            op0=ALU.add,
            op1=ALU.add,
        )

        result_flipped = psum.tile([P, 2, PAIR], F32, name="bank")
        nc.tensor.transpose(result_flipped[:, 0, 0:P], result[:], ident[:])
        out_rows = consts.tile([P, P], F32)
        nc.scalar.copy(out=out_rows[:], in_=result_flipped[:, 0, 0:P])
        nc.sync.dma_start(
            out=out.rearrange("b (t j) -> (b t) j", j=P),
            in_=out_rows[0 : BATCH * CHANNEL_TILES, :],
        )
